import numpy as np
import ml_dtypes

BF16 = ml_dtypes.bfloat16


def bf(x):
    return np.asarray(x, np.float32).astype(BF16)


def f32(x):
    return np.asarray(x, np.float32)


def f64(x):
    return np.asarray(x).astype(np.float64)


def striped(idx):
    return np.tile(idx.reshape(-1, 16).T, (8, 1))


D, C, N, S, T = 1024, 512, 1536, 3072, 3
SIG, BSC, WSC = 0.2, 0.05, 0.3


def setup_inputs():
    return {
        "xw": bf(np.random.standard_normal((D, N))),
        "w0": bf(SIG * np.random.standard_normal((D, C)) / np.sqrt(D)),
        "b0": f32(BSC * np.random.standard_normal((C, 1))),
        "w1": bf(np.random.standard_normal((C, C)) * np.sqrt(2.0 / C)),
        "b1": f32(BSC * np.random.standard_normal((C, 1))),
        "w2": bf(np.random.standard_normal((C, C)) * np.sqrt(2.0 / C)),
        "b2": f32(BSC * np.random.standard_normal((C, 1))),
        "base": f32(WSC * np.random.standard_normal((C, S))),
        "offs": striped(np.random.permutation(S)[:N]),
    }


def reference(xw, w0, b0, w1, b1, w2, b2, base, offs):
    idx = offs[:16].T.reshape(-1)
    l0 = np.maximum(f64(w0).T @ f64(xw) + f64(b0), 0.0)
    l1 = np.maximum(f64(w1).T @ l0 + f64(b1), 0.0)
    l2 = np.maximum(f64(w2).T @ l1 + f64(b2), 0.0)
    h = np.concatenate([l0, l1, l2], axis=1).reshape(C, N, T)
    sc = np.einsum("cni,cnt->nit", h, h) * (1.0 - np.eye(T))
    e = np.exp(sc - sc.max(axis=-1, keepdims=True))
    att = e / e.sum(axis=-1, keepdims=True)
    col = att.sum(axis=1)
    placed = (col[:, 0] * h[:, :, 0] + col[:, 1] * h[:, :, 1]) + col[:, 2] * h[:, :, 2]
    res = f64(base).copy()
    res[:, idx] = placed
    return res

@@ -1,0 +1,168 @@
+import concourse.masks as masks
+import concourse.mybir as mybir
+
+P = 128
+D, C, N, S, T = 1024, 512, 1536, 3072, 3
+LAYERS = 3
+KD = D // P
+KC = C // P
+JT = P
+W = T * JT
+U = N // W
+PAIRS = ((0, 1), (0, 2), (1, 2))
+
+FLOPS = 2 * N * C * (D + 2 * C) + 2 * len(PAIRS) * C * N + 5 * C * N
+
+BF16, F32, U16 = mybir.dt.bfloat16, mybir.dt.float32, mybir.dt.uint16
+ADD, SUBTRACT, MULT = mybir.AluOpType.add, mybir.AluOpType.subtract, mybir.AluOpType.mult
+RELU, EXP, COPY = (
+    mybir.ActivationFunctionType.Relu,
+    mybir.ActivationFunctionType.Exp,
+    mybir.ActivationFunctionType.Copy,
+)
+X = mybir.AxisListType.X
+
+
+def tile_safnn_b_kernel(tc, xw, w0, b0, w1, b1, w2, b2, base, offs, out):
+    nc = tc.nc
+    with (
+        tc.tile_pool(name="held", bufs=1) as held,
+        tc.tile_pool(name="hidden32", bufs=4) as hidden32,
+        tc.tile_pool(name="hidden16", bufs=6) as hidden16,
+        tc.tile_pool(name="products", bufs=3) as products,
+        tc.tile_pool(name="small", bufs=3) as small,
+        tc.tile_pool(name="wide", bufs=3) as wide,
+        tc.psum_pool(name="layer_psum", bufs=4) as layer_psum,
+        tc.psum_pool(name="score_psum", bufs=2) as score_psum,
+        tc.psum_pool(name="weight_psum", bufs=2) as weight_psum,
+    ):
+        offsets = held.tile([P, N // 16], U16, name="offsets")
+        nc.sync.dma_start(offsets[:], offs)
+
+        bias = []
+        with nc.allow_non_contiguous_dma(reason="a bias of 512 floats, one to a partition, four blocks side by side"):
+            for r, b in enumerate((b0, b1, b2)):
+                bias.append(held.tile([P, KC], F32, name=f"bias{r}"))
+                nc.gpsimd.dma_start(bias[r][:], b.rearrange("(m p) o -> p (m o)", p=P))
+
+        weights = [
+            held.tile([P, KD, C], BF16, name="weights0"),
+            held.tile([P, KC, C], BF16, name="weights1"),
+            held.tile([P, KC, C], BF16, name="weights2"),
+        ]
+        samples = [held.tile([P, KD, W], BF16, name=f"samples{u}") for u in range(U)]
+        xw_blocks = xw.rearrange("(k p) n -> p k n", p=P)
+
+        nc.scalar.dma_start(weights[0][:], w0.rearrange("(k p) c -> p k c", p=P))
+        nc.sync.dma_start(samples[0][:], xw_blocks[:, :, 0:W])
+        nc.sync.dma_start(samples[1][:], xw_blocks[:, :, W : 2 * W])
+        nc.sync.dma_start(weights[1][:], w1.rearrange("(k p) c -> p k c", p=P))
+        nc.sync.dma_start(samples[2][:], xw_blocks[:, :, 2 * W : 3 * W])
+        nc.sync.dma_start(weights[2][:], w2.rearrange("(k p) c -> p k c", p=P))
+        nc.sync.dma_start(samples[3][:], xw_blocks[:, :, 3 * W : 4 * W])
+
+        window = [held.tile([P, S], F32, name=f"window{m}") for m in range(KC)]
+        for m in range(KC):
+            nc.sync.dma_start(window[m][:], base[m * P : (m + 1) * P, :])
+
+        identity = held.tile([P, P], F32, name="identity")
+        masks.make_identity(nc, identity[:])
+        ones = held.tile([P, P], F32, name="ones")
+        nc.gpsimd.memset(ones[:], 1.0)
+        pair_places = held.tile([P, len(PAIRS), T * T], BF16, name="pair_places")
+        nc.gpsimd.memset(pair_places[:], 0.0)
+        for q, (i, t) in enumerate(PAIRS):
+            nc.gpsimd.memset(pair_places[:, q, T * i + t : T * i + t + 1], 1.0)
+            nc.gpsimd.memset(pair_places[:, q, T * t + i : T * t + i + 1], 1.0)
+
+        first_two = [held.tile([P, N], F32, name=f"first_two{m}") for m in range(KC)]
+        third = [held.tile([P, N], F32, name=f"third{m}") for m in range(KC)]
+
+        rounded = {}
+
+        def group(r, u):
+            moving = samples[u] if r == 0 else rounded[(r - 1, u)]
+            h32 = hidden32.tile([P, KC, T, JT], F32, name="h32")
+            if r < LAYERS - 1:
+                h16 = hidden16.tile([P, KC, W], BF16, name="h16")
+                rounded[(r, u)] = h16
+            order = "p (j t) -> p t j" if r == 0 else "p (t j) -> p t j"
+            blocks = KD if r == 0 else KC
+            for m in range(KC):
+                acc = layer_psum.tile([P, W], F32, name="acc")
+                for k in range(blocks):
+                    nc.tensor.matmul(
+                        acc[:],
+                        weights[r][:, k, m * P : (m + 1) * P],
+                        moving[:, k, :],
+                        start=(k == 0),
+                        stop=(k == blocks - 1),
+                    )
+                result = acc[:].rearrange(order, t=T)
+                nc.scalar.activation(h32[:, m, :, :], result, RELU, bias=bias[r][:, m : m + 1])
+                if r < LAYERS - 1:
+                    nc.scalar.activation(
+                        h16[:, m, :].rearrange("p (t j) -> p t j", t=T), result, RELU, bias=bias[r][:, m : m + 1]
+                    )
+
+            prod = products.tile([P, KC, len(PAIRS), JT], BF16, name="prod")
+            for m in range(KC):
+                nc.vector.tensor_tensor(
+                    prod[:, m, 0:2, :], h32[:, m, 0:1, :].to_broadcast([P, 2, JT]), h32[:, m, 1:3, :], MULT
+                )
+                nc.vector.tensor_tensor(prod[:, m, 2, :], h32[:, m, 1, :], h32[:, m, 2, :], MULT)
+            scores = score_psum.tile([P, T * T], F32, name="scores")
+            for m in range(KC):
+                for q in range(len(PAIRS)):
+                    nc.tensor.matmul(
+                        scores[:],
+                        prod[:, m, q, :],
+                        pair_places[:, q, :],
+                        start=(m == 0 and q == 0),
+                        stop=(m == KC - 1 and q == len(PAIRS) - 1),
+                    )
+
+            rows = scores[:].rearrange("p (i t) -> p i t", t=T)
+            top = small.tile([P, T], F32, name="top")
+            nc.vector.reduce_max(top[:], rows, axis=X)
+            shifted = small.tile([P, T, T], F32, name="shifted")
+            nc.vector.tensor_tensor(shifted[:], rows, top[:].unsqueeze(2).to_broadcast([P, T, T]), SUBTRACT)
+            expd = small.tile([P, T, T], F32, name="expd")
+            nc.scalar.activation(expd[:], shifted[:], EXP)
+            total = small.tile([P, T], F32, name="total")
+            nc.vector.reduce_sum(total[:], expd[:], axis=X)
+            inverse = small.tile([P, T], F32, name="inverse")
+            nc.vector.reciprocal(inverse[:], total[:])
+            att = small.tile([P, T, T], F32, name="att")
+            nc.vector.tensor_tensor(att[:], expd[:], inverse[:].unsqueeze(2).to_broadcast([P, T, T]), MULT)
+            col = small.tile([P, T], F32, name="col")
+            nc.vector.reduce_sum(col[:], att[:].rearrange("p i t -> p t i"), axis=X)
+
+            diagonal = wide.tile([P, T, JT], F32, name="diagonal")
+            for t in range(T):
+                nc.scalar.activation(diagonal[:, t, :], identity[:], COPY, scale=col[:, t : t + 1])
+            col_rows = weight_psum.tile([P, T, JT], F32, name="col_rows")
+            nc.tensor.matmul(
+                col_rows[:].rearrange("p t j -> p (t j)"),
+                ones[:],
+                diagonal[:].rearrange("p t j -> p (t j)"),
+                start=True,
+                stop=True,
+            )
+
+            entries = slice((r * U + u) * JT, (r * U + u + 1) * JT)
+            for m in range(KC):
+                two = wide.tile([P, 2, JT], F32, name="two")
+                nc.vector.tensor_tensor(two[:], col_rows[:, 0:2, :], h32[:, m, 0:2, :], MULT)
+                nc.vector.tensor_tensor(first_two[m][:, entries], two[:, 0, :], two[:, 1, :], ADD)
+                nc.vector.tensor_tensor(third[m][:, entries], col_rows[:, 2, :], h32[:, m, 2, :], MULT)
+
+        for diagonal_index in range(U + LAYERS - 1):
+            for r in range(LAYERS):
+                u = diagonal_index - r
+                if 0 <= u < U:
+                    group(r, u)
+
+        for m in range(KC):
+            nc.vector.tensor_tensor(window[m][:].indirect(offsets[:]), first_two[m][:], third[m][:], ADD)
+            nc.sync.dma_start(out[m * P : (m + 1) * P, :], window[m][:])

@@ -11,23 +11,49 @@ W = T * JT
 U = N // W
 PAIRS = ((0, 1), (0, 2), (1, 2))
 
+GROUPS = [(r, wave - r) for wave in range(U + LAYERS - 1) for r in range(LAYERS) if 0 <= wave - r < U]
+BLOCKS = len(GROUPS) * KC
+
+PRODUCTS_LAG = 1
+SCORES_LAG = 3
+SOFTMAX_LAG = 3
+SPREAD_LAG = 7
+WEIGHTED_LAG = SPREAD_LAG + KC - 1
+
 FLOPS = 2 * N * C * (D + 2 * C) + 2 * len(PAIRS) * C * N + 5 * C * N
 
 BF16, F32, U16 = mybir.dt.bfloat16, mybir.dt.float32, mybir.dt.uint16
 ADD, SUBTRACT, MULT = mybir.AluOpType.add, mybir.AluOpType.subtract, mybir.AluOpType.mult
-RELU, EXP, COPY = (
-    mybir.ActivationFunctionType.Relu,
-    mybir.ActivationFunctionType.Exp,
-    mybir.ActivationFunctionType.Copy,
-)
+RELU, EXP = mybir.ActivationFunctionType.Relu, mybir.ActivationFunctionType.Exp
 X = mybir.AxisListType.X
+
+SOFTMAX_TILES = {
+    "top": [P, T],
+    "shifted": [P, T, T],
+    "expd": [P, T, T],
+    "total": [P, T],
+    "inverse": [P, T],
+    "att": [P, T, T],
+    "col": [P, T],
+}
+
+
+def for_block(block, stage):
+    if 0 <= block < BLOCKS:
+        stage(*divmod(block, KC))
+
+
+def for_group_ending_at(block, stage):
+    g, m = divmod(block, KC)
+    if m == KC - 1 and 0 <= g < len(GROUPS):
+        stage(g)
 
 
 def tile_safnn_b_kernel(tc, xw, w0, b0, w1, b1, w2, b2, base, offs, out):
     nc = tc.nc
     with (
         tc.tile_pool(name="held", bufs=1) as held,
-        tc.tile_pool(name="hidden32", bufs=4) as hidden32,
+        tc.tile_pool(name="hidden32", bufs=5) as hidden32,
         tc.tile_pool(name="hidden16", bufs=6) as hidden16,
         tc.tile_pool(name="products", bufs=3) as products,
         tc.tile_pool(name="small", bufs=3) as small,
@@ -36,15 +62,6 @@ def tile_safnn_b_kernel(tc, xw, w0, b0, w1, b1, w2, b2, base, offs, out):
         tc.psum_pool(name="score_psum", bufs=2) as score_psum,
         tc.psum_pool(name="weight_psum", bufs=2) as weight_psum,
     ):
-        offsets = held.tile([P, N // 16], U16, name="offsets")
-        nc.sync.dma_start(offsets[:], offs)
-
-        bias = []
-        with nc.allow_non_contiguous_dma(reason="a bias of 512 floats, one to a partition, four blocks side by side"):
-            for r, b in enumerate((b0, b1, b2)):
-                bias.append(held.tile([P, KC], F32, name=f"bias{r}"))
-                nc.gpsimd.dma_start(bias[r][:], b.rearrange("(m p) o -> p (m o)", p=P))
-
         weights = [
             held.tile([P, KD, C], BF16, name="weights0"),
             held.tile([P, KC, C], BF16, name="weights1"),
@@ -53,22 +70,28 @@ def tile_safnn_b_kernel(tc, xw, w0, b0, w1, b1, w2, b2, base, offs, out):
         samples = [held.tile([P, KD, W], BF16, name=f"samples{u}") for u in range(U)]
         xw_blocks = xw.rearrange("(k p) n -> p k n", p=P)
 
-        nc.scalar.dma_start(weights[0][:], w0.rearrange("(k p) c -> p k c", p=P))
-        nc.sync.dma_start(samples[0][:], xw_blocks[:, :, 0:W])
+        for k in range(KD):
+            nc.scalar.dma_start(weights[0][:, k, :], w0[k * P : (k + 1) * P, :])
+            nc.sync.dma_start(samples[0][:, k, :], xw[k * P : (k + 1) * P, 0:W])
+        bias = []
+        with nc.allow_non_contiguous_dma(reason="a bias of 512 floats, one to a partition, four blocks side by side"):
+            for r, b in enumerate((b0, b1, b2)):
+                bias.append(held.tile([P, KC], F32, name=f"bias{r}"))
+                nc.sync.dma_start(bias[r][:], b.rearrange("(m p) o -> p (m o)", p=P))
         nc.sync.dma_start(samples[1][:], xw_blocks[:, :, W : 2 * W])
         nc.sync.dma_start(weights[1][:], w1.rearrange("(k p) c -> p k c", p=P))
         nc.sync.dma_start(samples[2][:], xw_blocks[:, :, 2 * W : 3 * W])
         nc.sync.dma_start(weights[2][:], w2.rearrange("(k p) c -> p k c", p=P))
         nc.sync.dma_start(samples[3][:], xw_blocks[:, :, 3 * W : 4 * W])
 
+        offsets = held.tile([P, N // 16], U16, name="offsets")
+        nc.sync.dma_start(offsets[:], offs)
         window = [held.tile([P, S], F32, name=f"window{m}") for m in range(KC)]
         for m in range(KC):
             nc.sync.dma_start(window[m][:], base[m * P : (m + 1) * P, :])
 
         identity = held.tile([P, P], F32, name="identity")
         masks.make_identity(nc, identity[:])
-        ones = held.tile([P, P], F32, name="ones")
-        nc.gpsimd.memset(ones[:], 1.0)
         pair_places = held.tile([P, len(PAIRS), T * T], BF16, name="pair_places")
         nc.gpsimd.memset(pair_places[:], 0.0)
         for q, (i, t) in enumerate(PAIRS):
@@ -78,90 +101,108 @@ def tile_safnn_b_kernel(tc, xw, w0, b0, w1, b1, w2, b2, base, offs, out):
         first_two = [held.tile([P, N], F32, name=f"first_two{m}") for m in range(KC)]
         third = [held.tile([P, N], F32, name=f"third{m}") for m in range(KC)]
 
-        rounded = {}
+        h32_of, h16_of, prod_of, scores_of, soft_of, col_rows_of, two_of = {}, {}, {}, {}, {}, {}, {}
 
-        def group(r, u):
-            moving = samples[u] if r == 0 else rounded[(r - 1, u)]
-            h32 = hidden32.tile([P, KC, T, JT], F32, name="h32")
-            if r < LAYERS - 1:
-                h16 = hidden16.tile([P, KC, W], BF16, name="h16")
-                rounded[(r, u)] = h16
-            order = "p (j t) -> p t j" if r == 0 else "p (t j) -> p t j"
-            blocks = KD if r == 0 else KC
-            for m in range(KC):
-                acc = layer_psum.tile([P, W], F32, name="acc")
-                for k in range(blocks):
-                    nc.tensor.matmul(
-                        acc[:],
-                        weights[r][:, k, m * P : (m + 1) * P],
-                        moving[:, k, :],
-                        start=(k == 0),
-                        stop=(k == blocks - 1),
-                    )
-                result = acc[:].rearrange(order, t=T)
-                nc.scalar.activation(h32[:, m, :, :], result, RELU, bias=bias[r][:, m : m + 1])
+        def layer_block(g, m):
+            r, u = GROUPS[g]
+            if m == 0:
+                h32_of[g] = hidden32.tile([P, KC, T, JT], F32, name="h32")
                 if r < LAYERS - 1:
-                    nc.scalar.activation(
-                        h16[:, m, :].rearrange("p (t j) -> p t j", t=T), result, RELU, bias=bias[r][:, m : m + 1]
-                    )
-
-            prod = products.tile([P, KC, len(PAIRS), JT], BF16, name="prod")
-            for m in range(KC):
-                nc.vector.tensor_tensor(
-                    prod[:, m, 0:2, :], h32[:, m, 0:1, :].to_broadcast([P, 2, JT]), h32[:, m, 1:3, :], MULT
+                    h16_of[(r, u)] = hidden16.tile([P, KC, T, JT], BF16, name="h16")
+            moving = samples[u] if r == 0 else h16_of[(r - 1, u)][:].rearrange("p k t j -> p k (t j)")
+            blocks = KD if r == 0 else KC
+            acc = layer_psum.tile([P, W], F32, name="acc")
+            for k in range(blocks):
+                nc.tensor.matmul(
+                    acc[:],
+                    weights[r][:, k, m * P : (m + 1) * P],
+                    moving[:, k, :],
+                    start=(k == 0),
+                    stop=(k == blocks - 1),
                 )
-                nc.vector.tensor_tensor(prod[:, m, 2, :], h32[:, m, 1, :], h32[:, m, 2, :], MULT)
-            scores = score_psum.tile([P, T * T], F32, name="scores")
+            result = acc[:].rearrange("p (j t) -> p t j" if r == 0 else "p (t j) -> p t j", t=T)
+            nc.scalar.activation(h32_of[g][:, m, :, :], result, RELU, bias=bias[r][:, m : m + 1])
+            if r < LAYERS - 1:
+                nc.scalar.activation(h16_of[(r, u)][:, m, :, :], result, RELU, bias=bias[r][:, m : m + 1])
+
+        def pair_products(g, m):
+            if m == 0:
+                prod_of[g] = products.tile([P, KC, len(PAIRS), JT], BF16, name="prod")
+            h32, prod = h32_of[g], prod_of[g]
+            nc.gpsimd.tensor_tensor(
+                prod[:, m, 0:2, :], h32[:, m, 0:1, :].to_broadcast([P, 2, JT]), h32[:, m, 1:3, :], MULT
+            )
+            nc.vector.tensor_tensor(prod[:, m, 2, :], h32[:, m, 1, :], h32[:, m, 2, :], MULT)
+
+        def scores(g):
+            scores_of[g] = score_psum.tile([P, T, T], F32, name="scores")
             for m in range(KC):
                 for q in range(len(PAIRS)):
                     nc.tensor.matmul(
-                        scores[:],
-                        prod[:, m, q, :],
+                        scores_of[g][:].rearrange("p i t -> p (i t)"),
+                        prod_of[g][:, m, q, :],
                         pair_places[:, q, :],
                         start=(m == 0 and q == 0),
                         stop=(m == KC - 1 and q == len(PAIRS) - 1),
                     )
 
-            rows = scores[:].rearrange("p (i t) -> p i t", t=T)
-            top = small.tile([P, T], F32, name="top")
-            nc.vector.reduce_max(top[:], rows, axis=X)
-            shifted = small.tile([P, T, T], F32, name="shifted")
-            nc.vector.tensor_tensor(shifted[:], rows, top[:].unsqueeze(2).to_broadcast([P, T, T]), SUBTRACT)
-            expd = small.tile([P, T, T], F32, name="expd")
-            nc.scalar.activation(expd[:], shifted[:], EXP)
-            total = small.tile([P, T], F32, name="total")
-            nc.vector.reduce_sum(total[:], expd[:], axis=X)
-            inverse = small.tile([P, T], F32, name="inverse")
-            nc.vector.reciprocal(inverse[:], total[:])
-            att = small.tile([P, T, T], F32, name="att")
-            nc.vector.tensor_tensor(att[:], expd[:], inverse[:].unsqueeze(2).to_broadcast([P, T, T]), MULT)
-            col = small.tile([P, T], F32, name="col")
-            nc.vector.reduce_sum(col[:], att[:].rearrange("p i t -> p t i"), axis=X)
+        def row_maxima(g):
+            soft_of[g] = {name: small.tile(shape, F32, name=name) for name, shape in SOFTMAX_TILES.items()}
+            nc.vector.reduce_max(soft_of[g]["top"][:], scores_of[g][:], axis=X)
 
-            diagonal = wide.tile([P, T, JT], F32, name="diagonal")
+        def shift_and_exp(g):
+            soft = soft_of[g]
+            top_of_row = soft["top"][:].unsqueeze(2).to_broadcast([P, T, T])
+            nc.vector.tensor_tensor(soft["shifted"][:], scores_of[g][:], top_of_row, SUBTRACT)
+            nc.scalar.activation(soft["expd"][:], soft["shifted"][:], EXP)
+
+        def row_sums(g):
+            nc.vector.reduce_sum(soft_of[g]["total"][:], soft_of[g]["expd"][:], axis=X)
+
+        def row_inverses(g):
+            nc.vector.reciprocal(soft_of[g]["inverse"][:], soft_of[g]["total"][:])
+
+        def attention(g):
+            soft = soft_of[g]
+            inverse_of_row = soft["inverse"][:].unsqueeze(2).to_broadcast([P, T, T])
+            nc.vector.tensor_tensor(soft["att"][:], soft["expd"][:], inverse_of_row, MULT)
+
+        def column_sums(g):
+            nc.vector.reduce_sum(soft_of[g]["col"][:], soft_of[g]["att"][:].rearrange("p i t -> p t i"), axis=X)
+
+        def spread(g):
+            col_rows_of[g] = weight_psum.tile([P, T, JT], F32, name="col_rows")
+            col = soft_of[g]["col"]
             for t in range(T):
-                nc.scalar.activation(diagonal[:, t, :], identity[:], COPY, scale=col[:, t : t + 1])
-            col_rows = weight_psum.tile([P, T, JT], F32, name="col_rows")
-            nc.tensor.matmul(
-                col_rows[:].rearrange("p t j -> p (t j)"),
-                ones[:],
-                diagonal[:].rearrange("p t j -> p (t j)"),
-                start=True,
-                stop=True,
-            )
+                nc.tensor.transpose(col_rows_of[g][:, t, :], col[:, t : t + 1].to_broadcast([P, P]), identity[:])
 
-            entries = slice((r * U + u) * JT, (r * U + u + 1) * JT)
-            for m in range(KC):
-                two = wide.tile([P, 2, JT], F32, name="two")
-                nc.vector.tensor_tensor(two[:], col_rows[:, 0:2, :], h32[:, m, 0:2, :], MULT)
-                nc.vector.tensor_tensor(first_two[m][:, entries], two[:, 0, :], two[:, 1, :], ADD)
-                nc.vector.tensor_tensor(third[m][:, entries], col_rows[:, 2, :], h32[:, m, 2, :], MULT)
+        def entries_of(g):
+            r, u = GROUPS[g]
+            return slice((r * U + u) * JT, (r * U + u + 1) * JT)
 
-        for diagonal_index in range(U + LAYERS - 1):
-            for r in range(LAYERS):
-                u = diagonal_index - r
-                if 0 <= u < U:
-                    group(r, u)
+        def weighted_products(g, m):
+            h32, col_rows = h32_of[g], col_rows_of[g]
+            two_of[(g, m)] = wide.tile([P, 2, JT], F32, name="two")
+            nc.vector.tensor_tensor(two_of[(g, m)][:], col_rows[:, 0:2, :], h32[:, m, 0:2, :], MULT)
+            nc.vector.tensor_tensor(third[m][:, entries_of(g)], col_rows[:, 2, :], h32[:, m, 2, :], MULT)
+
+        def weighted_sum(g, m):
+            two = two_of[(g, m)]
+            nc.vector.tensor_tensor(first_two[m][:, entries_of(g)], two[:, 0, :], two[:, 1, :], ADD)
+
+        for turn in range(BLOCKS + WEIGHTED_LAG):
+            for_group_ending_at(turn - SPREAD_LAG, spread)
+            for_group_ending_at(turn - SCORES_LAG, scores)
+            for_group_ending_at(turn - SOFTMAX_LAG, row_maxima)
+            for_group_ending_at(turn - SOFTMAX_LAG - 1, row_sums)
+            for_group_ending_at(turn - SOFTMAX_LAG - 2, attention)
+            for_block(turn - WEIGHTED_LAG, weighted_products)
+            for_group_ending_at(turn - SOFTMAX_LAG, shift_and_exp)
+            for_group_ending_at(turn - SOFTMAX_LAG - 1, row_inverses)
+            for_group_ending_at(turn - SOFTMAX_LAG - 2, column_sums)
+            for_block(turn - WEIGHTED_LAG, weighted_sum)
+            for_block(turn - PRODUCTS_LAG, pair_products)
+            for_block(turn, layer_block)
 
         for m in range(KC):
             nc.vector.tensor_tensor(window[m][:].indirect(offsets[:]), first_two[m][:], third[m][:], ADD)

@@ -129,10 +129,11 @@ def tile_safnn_b_kernel(tc, xw, w0, b0, w1, b1, w2, b2, base, offs, out):
             if m == 0:
                 prod_of[g] = products.tile([P, KC, len(PAIRS), JT], BF16, name="prod")
             h32, prod = h32_of[g], prod_of[g]
-            nc.gpsimd.tensor_tensor(
+            engine = nc.gpsimd if m == 0 else nc.vector
+            engine.tensor_tensor(
                 prod[:, m, 0:2, :], h32[:, m, 0:1, :].to_broadcast([P, 2, JT]), h32[:, m, 1:3, :], MULT
             )
-            nc.vector.tensor_tensor(prod[:, m, 2, :], h32[:, m, 1, :], h32[:, m, 2, :], MULT)
+            engine.tensor_tensor(prod[:, m, 2, :], h32[:, m, 1, :], h32[:, m, 2, :], MULT)
 
         def scores(g):
             scores_of[g] = score_psum.tile([P, T, T], F32, name="scores")

@@ -19,6 +19,7 @@ SCORES_LAG = 3
 SOFTMAX_LAG = 3
 SPREAD_LAG = 7
 WEIGHTED_LAG = SPREAD_LAG + KC - 1
+SUM_LAG = WEIGHTED_LAG + 1
 
 FLOPS = 2 * N * C * (D + 2 * C) + 2 * len(PAIRS) * C * N + 5 * C * N
 
@@ -129,11 +130,10 @@ def tile_safnn_b_kernel(tc, xw, w0, b0, w1, b1, w2, b2, base, offs, out):
             if m == 0:
                 prod_of[g] = products.tile([P, KC, len(PAIRS), JT], BF16, name="prod")
             h32, prod = h32_of[g], prod_of[g]
-            engine = nc.gpsimd if m == 0 else nc.vector
-            engine.tensor_tensor(
+            nc.vector.tensor_tensor(
                 prod[:, m, 0:2, :], h32[:, m, 0:1, :].to_broadcast([P, 2, JT]), h32[:, m, 1:3, :], MULT
             )
-            engine.tensor_tensor(prod[:, m, 2, :], h32[:, m, 1, :], h32[:, m, 2, :], MULT)
+            nc.vector.tensor_tensor(prod[:, m, 2, :], h32[:, m, 1, :], h32[:, m, 2, :], MULT)
 
         def scores(g):
             scores_of[g] = score_psum.tile([P, T, T], F32, name="scores")
@@ -191,7 +191,7 @@ def tile_safnn_b_kernel(tc, xw, w0, b0, w1, b1, w2, b2, base, offs, out):
             two = two_of[(g, m)]
             nc.vector.tensor_tensor(first_two[m][:, entries_of(g)], two[:, 0, :], two[:, 1, :], ADD)
 
-        for turn in range(BLOCKS + WEIGHTED_LAG):
+        for turn in range(BLOCKS + SUM_LAG):
             for_group_ending_at(turn - SPREAD_LAG, spread)
             for_group_ending_at(turn - SCORES_LAG, scores)
             for_group_ending_at(turn - SOFTMAX_LAG, row_maxima)
@@ -201,7 +201,7 @@ def tile_safnn_b_kernel(tc, xw, w0, b0, w1, b1, w2, b2, base, offs, out):
             for_group_ending_at(turn - SOFTMAX_LAG, shift_and_exp)
             for_group_ending_at(turn - SOFTMAX_LAG - 1, row_inverses)
             for_group_ending_at(turn - SOFTMAX_LAG - 2, column_sums)
-            for_block(turn - WEIGHTED_LAG, weighted_sum)
+            for_block(turn - SUM_LAG, weighted_sum)
             for_block(turn - PRODUCTS_LAG, pair_products)
             for_block(turn, layer_block)
 

@@ -17,7 +17,7 @@ BLOCKS = len(GROUPS) * KC
 PRODUCTS_LAG = 1
 SCORES_LAG = 3
 SOFTMAX_LAG = 3
-SPREAD_LAG = 7
+SPREAD_LAG = 5
 WEIGHTED_LAG = SPREAD_LAG + KC - 1
 SUM_LAG = WEIGHTED_LAG + 1
 
@@ -29,11 +29,8 @@ RELU, EXP = mybir.ActivationFunctionType.Relu, mybir.ActivationFunctionType.Exp
 X = mybir.AxisListType.X
 
 SOFTMAX_TILES = {
-    "top": [P, T],
-    "shifted": [P, T, T],
-    "expd": [P, T, T],
-    "total": [P, T],
-    "inverse": [P, T],
+    "expd": [P, T, T, T],
+    "total": [P, T, T],
     "att": [P, T, T],
     "col": [P, T],
 }
@@ -98,6 +95,14 @@ def tile_safnn_b_kernel(tc, xw, w0, b0, w1, b1, w2, b2, base, offs, out):
         for q, (i, t) in enumerate(PAIRS):
             nc.gpsimd.memset(pair_places[:, q, T * i + t : T * i + t + 1], 1.0)
             nc.gpsimd.memset(pair_places[:, q, T * t + i : T * t + i + 1], 1.0)
+        difference_places = held.tile([P, len(PAIRS) * T, T, T], BF16, name="difference_places")
+        places_by_row = pair_places[:].rearrange("p q (i u) -> p (q i) u", u=T)
+        nc.gpsimd.tensor_tensor(
+            difference_places[:],
+            places_by_row.unsqueeze(2).to_broadcast([P, len(PAIRS) * T, T, T]),
+            places_by_row.unsqueeze(3).to_broadcast([P, len(PAIRS) * T, T, T]),
+            SUBTRACT,
+        )
 
         first_two = [held.tile([P, N], F32, name=f"first_two{m}") for m in range(KC)]
         third = [held.tile([P, N], F32, name=f"third{m}") for m in range(KC)]
@@ -136,37 +141,26 @@ def tile_safnn_b_kernel(tc, xw, w0, b0, w1, b1, w2, b2, base, offs, out):
             nc.vector.tensor_tensor(prod[:, m, 2, :], h32[:, m, 1, :], h32[:, m, 2, :], MULT)
 
         def scores(g):
-            scores_of[g] = score_psum.tile([P, T, T], F32, name="scores")
+            scores_of[g] = score_psum.tile([P, T, T, T], F32, name="scores")
             for m in range(KC):
                 for q in range(len(PAIRS)):
                     nc.tensor.matmul(
-                        scores_of[g][:].rearrange("p i t -> p (i t)"),
+                        scores_of[g][:].rearrange("p i t u -> p (i t u)"),
                         prod_of[g][:, m, q, :],
-                        pair_places[:, q, :],
+                        difference_places[:, q * T : (q + 1) * T, :, :].rearrange("p i t u -> p (i t u)"),
                         start=(m == 0 and q == 0),
                         stop=(m == KC - 1 and q == len(PAIRS) - 1),
                     )
 
-        def row_maxima(g):
+        def exponentials(g):
             soft_of[g] = {name: small.tile(shape, F32, name=name) for name, shape in SOFTMAX_TILES.items()}
-            nc.vector.reduce_max(soft_of[g]["top"][:], scores_of[g][:], axis=X)
+            nc.scalar.activation(soft_of[g]["expd"][:], scores_of[g][:], EXP)
 
-        def shift_and_exp(g):
-            soft = soft_of[g]
-            top_of_row = soft["top"][:].unsqueeze(2).to_broadcast([P, T, T])
-            nc.vector.tensor_tensor(soft["shifted"][:], scores_of[g][:], top_of_row, SUBTRACT)
-            nc.scalar.activation(soft["expd"][:], soft["shifted"][:], EXP)
-
-        def row_sums(g):
+        def denominators(g):
             nc.vector.reduce_sum(soft_of[g]["total"][:], soft_of[g]["expd"][:], axis=X)
 
-        def row_inverses(g):
-            nc.vector.reciprocal(soft_of[g]["inverse"][:], soft_of[g]["total"][:])
-
         def attention(g):
-            soft = soft_of[g]
-            inverse_of_row = soft["inverse"][:].unsqueeze(2).to_broadcast([P, T, T])
-            nc.vector.tensor_tensor(soft["att"][:], soft["expd"][:], inverse_of_row, MULT)
+            nc.vector.reciprocal(soft_of[g]["att"][:], soft_of[g]["total"][:])
 
         def column_sums(g):
             nc.vector.reduce_sum(soft_of[g]["col"][:], soft_of[g]["att"][:].rearrange("p i t -> p t i"), axis=X)
@@ -194,13 +188,11 @@ def tile_safnn_b_kernel(tc, xw, w0, b0, w1, b1, w2, b2, base, offs, out):
         for turn in range(BLOCKS + SUM_LAG):
             for_group_ending_at(turn - SPREAD_LAG, spread)
             for_group_ending_at(turn - SCORES_LAG, scores)
-            for_group_ending_at(turn - SOFTMAX_LAG, row_maxima)
-            for_group_ending_at(turn - SOFTMAX_LAG - 1, row_sums)
-            for_group_ending_at(turn - SOFTMAX_LAG - 2, attention)
+            for_group_ending_at(turn - SOFTMAX_LAG, exponentials)
+            for_group_ending_at(turn - SOFTMAX_LAG - 1, attention)
             for_block(turn - WEIGHTED_LAG, weighted_products)
-            for_group_ending_at(turn - SOFTMAX_LAG, shift_and_exp)
-            for_group_ending_at(turn - SOFTMAX_LAG - 1, row_inverses)
-            for_group_ending_at(turn - SOFTMAX_LAG - 2, column_sums)
+            for_group_ending_at(turn - SOFTMAX_LAG, denominators)
+            for_group_ending_at(turn - SOFTMAX_LAG - 1, column_sums)
             for_block(turn - SUM_LAG, weighted_sum)
             for_block(turn - PRODUCTS_LAG, pair_products)
             for_block(turn, layer_block)

@@ -17,7 +17,7 @@ BLOCKS = len(GROUPS) * KC
 PRODUCTS_LAG = 1
 SCORES_LAG = 3
 SOFTMAX_LAG = 3
-SPREAD_LAG = 5
+SPREAD_LAG = 7
 WEIGHTED_LAG = SPREAD_LAG + KC - 1
 SUM_LAG = WEIGHTED_LAG + 1
 

@@ -15,9 +15,9 @@ GROUPS = [(r, wave - r) for wave in range(U + LAYERS - 1) for r in range(LAYERS)
 BLOCKS = len(GROUPS) * KC
 
 PRODUCTS_LAG = 1
-SCORES_LAG = 3
-SOFTMAX_LAG = 3
-SPREAD_LAG = 7
+SCORES_LAG = 4
+SOFTMAX_LAG = 4
+SPREAD_LAG = 8
 WEIGHTED_LAG = SPREAD_LAG + KC - 1
 SUM_LAG = WEIGHTED_LAG + 1
 
@@ -51,11 +51,10 @@ def tile_safnn_b_kernel(tc, xw, w0, b0, w1, b1, w2, b2, base, offs, out):
     nc = tc.nc
     with (
         tc.tile_pool(name="held", bufs=1) as held,
-        tc.tile_pool(name="hidden32", bufs=5) as hidden32,
+        tc.tile_pool(name="hidden32", bufs=6) as hidden32,
         tc.tile_pool(name="hidden16", bufs=6) as hidden16,
         tc.tile_pool(name="products", bufs=3) as products,
         tc.tile_pool(name="small", bufs=3) as small,
-        tc.tile_pool(name="wide", bufs=3) as wide,
         tc.psum_pool(name="layer_psum", bufs=4) as layer_psum,
         tc.psum_pool(name="score_psum", bufs=2) as score_psum,
         tc.psum_pool(name="weight_psum", bufs=2) as weight_psum,
@@ -104,10 +103,9 @@ def tile_safnn_b_kernel(tc, xw, w0, b0, w1, b1, w2, b2, base, offs, out):
             SUBTRACT,
         )
 
-        first_two = [held.tile([P, N], F32, name=f"first_two{m}") for m in range(KC)]
-        third = [held.tile([P, N], F32, name=f"third{m}") for m in range(KC)]
+        weighted = held.tile([P, KC, T, N], F32, name="weighted")
 
-        h32_of, h16_of, prod_of, scores_of, soft_of, col_rows_of, two_of = {}, {}, {}, {}, {}, {}, {}
+        h32_of, h16_of, prod_of, scores_of, soft_of, col_rows_of = {}, {}, {}, {}, {}, {}
 
         def layer_block(g, m):
             r, u = GROUPS[g]
@@ -176,14 +174,11 @@ def tile_safnn_b_kernel(tc, xw, w0, b0, w1, b1, w2, b2, base, offs, out):
             return slice((r * U + u) * JT, (r * U + u + 1) * JT)
 
         def weighted_products(g, m):
-            h32, col_rows = h32_of[g], col_rows_of[g]
-            two_of[(g, m)] = wide.tile([P, 2, JT], F32, name="two")
-            nc.vector.tensor_tensor(two_of[(g, m)][:], col_rows[:, 0:2, :], h32[:, m, 0:2, :], MULT)
-            nc.vector.tensor_tensor(third[m][:, entries_of(g)], col_rows[:, 2, :], h32[:, m, 2, :], MULT)
+            nc.vector.tensor_tensor(weighted[:, m, :, entries_of(g)], col_rows_of[g][:], h32_of[g][:, m, :, :], MULT)
 
-        def weighted_sum(g, m):
-            two = two_of[(g, m)]
-            nc.vector.tensor_tensor(first_two[m][:, entries_of(g)], two[:, 0, :], two[:, 1, :], ADD)
+        def weighted_sum(g):
+            first, second = weighted[:, :, 0, entries_of(g)], weighted[:, :, 1, entries_of(g)]
+            nc.vector.tensor_tensor(first, first, second, ADD)
 
         for turn in range(BLOCKS + SUM_LAG):
             for_group_ending_at(turn - SPREAD_LAG, spread)
@@ -193,10 +188,10 @@ def tile_safnn_b_kernel(tc, xw, w0, b0, w1, b1, w2, b2, base, offs, out):
             for_block(turn - WEIGHTED_LAG, weighted_products)
             for_group_ending_at(turn - SOFTMAX_LAG, denominators)
             for_group_ending_at(turn - SOFTMAX_LAG - 1, column_sums)
-            for_block(turn - SUM_LAG, weighted_sum)
+            for_group_ending_at(turn - SUM_LAG, weighted_sum)
             for_block(turn - PRODUCTS_LAG, pair_products)
             for_block(turn, layer_block)
 
         for m in range(KC):
-            nc.vector.tensor_tensor(window[m][:].indirect(offsets[:]), first_two[m][:], third[m][:], ADD)
+            nc.vector.tensor_tensor(window[m][:].indirect(offsets[:]), weighted[:, m, 0, :], weighted[:, m, 2, :], ADD)
             nc.sync.dma_start(out[m * P : (m + 1) * P, :], window[m][:])

@@ -55,8 +55,8 @@ def tile_safnn_b_kernel(tc, xw, w0, b0, w1, b1, w2, b2, base, offs, out):
         tc.tile_pool(name="hidden16", bufs=6) as hidden16,
         tc.tile_pool(name="products", bufs=3) as products,
         tc.tile_pool(name="small", bufs=3) as small,
-        tc.psum_pool(name="layer_psum", bufs=4) as layer_psum,
-        tc.psum_pool(name="score_psum", bufs=2) as score_psum,
+        tc.psum_pool(name="layer_psum", bufs=5) as layer_psum,
+        tc.psum_pool(name="score_psum", bufs=1) as score_psum,
         tc.psum_pool(name="weight_psum", bufs=2) as weight_psum,
     ):
         weights = [
@@ -67,14 +67,17 @@ def tile_safnn_b_kernel(tc, xw, w0, b0, w1, b1, w2, b2, base, offs, out):
         samples = [held.tile([P, KD, W], BF16, name=f"samples{u}") for u in range(U)]
         xw_blocks = xw.rearrange("(k p) n -> p k n", p=P)
 
-        for k in range(KD):
-            nc.scalar.dma_start(weights[0][:, k, :], w0[k * P : (k + 1) * P, :])
-            nc.sync.dma_start(samples[0][:, k, :], xw[k * P : (k + 1) * P, 0:W])
         bias = []
         with nc.allow_non_contiguous_dma(reason="a bias of 512 floats, one to a partition, four blocks side by side"):
             for r, b in enumerate((b0, b1, b2)):
                 bias.append(held.tile([P, KC], F32, name=f"bias{r}"))
-                nc.sync.dma_start(bias[r][:], b.rearrange("(m p) o -> p (m o)", p=P))
+                nc.gpsimd.dma_start(bias[r][:], b.rearrange("(m p) o -> p (m o)", p=P))
+        for k in range(KD):
+            nc.scalar.dma_start(weights[0][:, k, :], w0[k * P : (k + 1) * P, :])
+            nc.sync.dma_start(samples[0][:, k, :], xw[k * P : (k + 1) * P, 0:W])
+        table_warmer = held.tile([P, 1], F32, name="table_warmer")
+        nc.gpsimd.memset(table_warmer[:], 0.0)
+        nc.scalar.activation(table_warmer[:], table_warmer[:], EXP)
         nc.sync.dma_start(samples[1][:], xw_blocks[:, :, W : 2 * W])
         nc.sync.dma_start(weights[1][:], w1.rearrange("(k p) c -> p k c", p=P))
         nc.sync.dma_start(samples[2][:], xw_blocks[:, :, 2 * W : 3 * W])
@@ -107,27 +110,38 @@ def tile_safnn_b_kernel(tc, xw, w0, b0, w1, b1, w2, b2, base, offs, out):
 
         h32_of, h16_of, prod_of, scores_of, soft_of, col_rows_of = {}, {}, {}, {}, {}, {}
 
-        def layer_block(g, m):
+        def multiply(g, m, acc, k):
+            r, u = GROUPS[g]
+            moving = samples[u] if r == 0 else h16_of[(r - 1, u)][:].rearrange("p k t j -> p k (t j)")
+            last = (KD if r == 0 else KC) - 1
+            nc.tensor.matmul(
+                acc[:], weights[r][:, k, m * P : (m + 1) * P], moving[:, k, :], start=(k == 0), stop=(k == last)
+            )
+
+        def bias_and_relu(g, m, acc):
             r, u = GROUPS[g]
             if m == 0:
                 h32_of[g] = hidden32.tile([P, KC, T, JT], F32, name="h32")
                 if r < LAYERS - 1:
                     h16_of[(r, u)] = hidden16.tile([P, KC, T, JT], BF16, name="h16")
-            moving = samples[u] if r == 0 else h16_of[(r - 1, u)][:].rearrange("p k t j -> p k (t j)")
-            blocks = KD if r == 0 else KC
-            acc = layer_psum.tile([P, W], F32, name="acc")
-            for k in range(blocks):
-                nc.tensor.matmul(
-                    acc[:],
-                    weights[r][:, k, m * P : (m + 1) * P],
-                    moving[:, k, :],
-                    start=(k == 0),
-                    stop=(k == blocks - 1),
-                )
             result = acc[:].rearrange("p (j t) -> p t j" if r == 0 else "p (t j) -> p t j", t=T)
             nc.scalar.activation(h32_of[g][:, m, :, :], result, RELU, bias=bias[r][:, m : m + 1])
             if r < LAYERS - 1:
                 nc.scalar.activation(h16_of[(r, u)][:, m, :, :], result, RELU, bias=bias[r][:, m : m + 1])
+
+        def layer_block(g, m):
+            acc = layer_psum.tile([P, W], F32, name="acc")
+            for k in range(KD if GROUPS[g][0] == 0 else KC):
+                multiply(g, m, acc, k)
+            bias_and_relu(g, m, acc)
+
+        def first_group():
+            accs = [layer_psum.tile([P, W], F32, name="acc") for m in range(KC)]
+            for k in range(KD):
+                for m in range(KC):
+                    multiply(0, m, accs[m], k)
+            for m in range(KC):
+                bias_and_relu(0, m, accs[m])
 
         def pair_products(g, m):
             if m == 0:
@@ -185,12 +199,15 @@ def tile_safnn_b_kernel(tc, xw, w0, b0, w1, b1, w2, b2, base, offs, out):
             for_group_ending_at(turn - SCORES_LAG, scores)
             for_group_ending_at(turn - SOFTMAX_LAG, exponentials)
             for_group_ending_at(turn - SOFTMAX_LAG - 1, attention)
-            for_block(turn - WEIGHTED_LAG, weighted_products)
-            for_group_ending_at(turn - SOFTMAX_LAG, denominators)
-            for_group_ending_at(turn - SOFTMAX_LAG - 1, column_sums)
             for_group_ending_at(turn - SUM_LAG, weighted_sum)
             for_block(turn - PRODUCTS_LAG, pair_products)
-            for_block(turn, layer_block)
+            for_group_ending_at(turn - SOFTMAX_LAG, denominators)
+            for_group_ending_at(turn - SOFTMAX_LAG - 1, column_sums)
+            for_block(turn - WEIGHTED_LAG, weighted_products)
+            if turn == 0:
+                first_group()
+            elif turn >= KC:
+                for_block(turn, layer_block)
 
         for m in range(KC):
             nc.vector.tensor_tensor(window[m][:].indirect(offsets[:]), weighted[:, m, 0, :], weighted[:, m, 2, :], ADD)

@@ -78,7 +78,8 @@ def tile_safnn_b_kernel(tc, xw, w0, b0, w1, b1, w2, b2, base, offs, out):
         table_warmer = held.tile([P, 1], F32, name="table_warmer")
         nc.gpsimd.memset(table_warmer[:], 0.0)
         nc.scalar.activation(table_warmer[:], table_warmer[:], EXP)
-        nc.sync.dma_start(samples[1][:], xw_blocks[:, :, W : 2 * W])
+        for k in range(KD):
+            nc.sync.dma_start(samples[1][:, k, :], xw[k * P : (k + 1) * P, W : 2 * W])
         nc.sync.dma_start(weights[1][:], w1.rearrange("(k p) c -> p k c", p=P))
         nc.sync.dma_start(samples[2][:], xw_blocks[:, :, 2 * W : 3 * W])
         nc.sync.dma_start(weights[2][:], w2.rearrange("(k p) c -> p k c", p=P))

@@ -21,11 +21,14 @@ SPREAD_LAG = 8
 WEIGHTED_LAG = SPREAD_LAG + KC - 1
 SUM_LAG = WEIGHTED_LAG + 1
 
+LATE_GROUPS = range(len(GROUPS) - U, len(GROUPS))
+
 FLOPS = 2 * N * C * (D + 2 * C) + 2 * len(PAIRS) * C * N + 5 * C * N
 
 BF16, F32, U16 = mybir.dt.bfloat16, mybir.dt.float32, mybir.dt.uint16
 ADD, SUBTRACT, MULT = mybir.AluOpType.add, mybir.AluOpType.subtract, mybir.AluOpType.mult
 RELU, EXP = mybir.ActivationFunctionType.Relu, mybir.ActivationFunctionType.Exp
+COPY = mybir.ActivationFunctionType.Copy
 X = mybir.AxisListType.X
 
 SOFTMAX_TILES = {
@@ -54,7 +57,8 @@ def tile_safnn_b_kernel(tc, xw, w0, b0, w1, b1, w2, b2, base, offs, out):
         tc.tile_pool(name="hidden32", bufs=6) as hidden32,
         tc.tile_pool(name="hidden16", bufs=6) as hidden16,
         tc.tile_pool(name="products", bufs=3) as products,
-        tc.tile_pool(name="small", bufs=3) as small,
+        tc.tile_pool(name="small", bufs=len(LATE_GROUPS) + 1) as small,
+        tc.tile_pool(name="turned", bufs=3) as turned,
         tc.psum_pool(name="layer_psum", bufs=5) as layer_psum,
         tc.psum_pool(name="score_psum", bufs=1) as score_psum,
         tc.psum_pool(name="weight_psum", bufs=2) as weight_psum,
@@ -188,11 +192,17 @@ def tile_safnn_b_kernel(tc, xw, w0, b0, w1, b1, w2, b2, base, offs, out):
             r, u = GROUPS[g]
             return slice((r * U + u) * JT, (r * U + u + 1) * JT)
 
+        def on_vector(g, m):
+            return m == 0 or g not in LATE_GROUPS
+
         def weighted_products(g, m):
+            if not on_vector(g, m):
+                return
             nc.vector.tensor_tensor(weighted[:, m, :, entries_of(g)], col_rows_of[g][:], h32_of[g][:, m, :, :], MULT)
 
         def weighted_sum(g):
-            first, second = weighted[:, :, 0, entries_of(g)], weighted[:, :, 1, entries_of(g)]
+            blocks = slice(0, 1) if g in LATE_GROUPS else slice(0, KC)
+            first, second = weighted[:, blocks, 0, entries_of(g)], weighted[:, blocks, 1, entries_of(g)]
             nc.vector.tensor_tensor(first, first, second, ADD)
 
         for turn in range(BLOCKS + SUM_LAG):
@@ -209,6 +219,33 @@ def tile_safnn_b_kernel(tc, xw, w0, b0, w1, b1, w2, b2, base, offs, out):
                 first_group()
             elif turn >= KC:
                 for_block(turn, layer_block)
+
+        scaled_of = {}
+
+        def turn_and_scale(g, m):
+            rows = layer_psum.tile([P, T, P], F32, name="rows", tag="acc")
+            for t in range(T):
+                nc.tensor.transpose(rows[:, t, :], h32_of[g][:, m, t, :], identity[:])
+            scaled_of[(g, m)] = turned.tile([P, T, P], F32, name="scaled")
+            for t in range(T):
+                nc.scalar.activation(
+                    scaled_of[(g, m)][:, t, :], rows[:, t, :], COPY, scale=soft_of[g]["col"][:, t : t + 1]
+                )
+
+        def turn_back_and_add(g, m):
+            sums = layer_psum.tile([P, 2, JT], F32, name="sums", tag="acc")
+            scaled = scaled_of[(g, m)]
+            nc.tensor.matmul(sums[:, 0, :], scaled[:, 0, :], identity[:], start=True, stop=False)
+            nc.tensor.matmul(sums[:, 0, :], scaled[:, 1, :], identity[:], start=False, stop=True)
+            nc.tensor.matmul(sums[:, 1, :], scaled[:, 2, :], identity[:], start=True, stop=True)
+            nc.scalar.activation(weighted[:, m, 0::2, entries_of(g)], sums[:], COPY)
+
+        late_blocks = [(g, m) for m in range(1, KC) for g in LATE_GROUPS]
+        for i in range(len(late_blocks) + 1):
+            if i < len(late_blocks):
+                turn_and_scale(*late_blocks[i])
+            if i > 0:
+                turn_back_and_add(*late_blocks[i - 1])
 
         for m in range(KC):
             nc.vector.tensor_tensor(window[m][:].indirect(offsets[:]), weighted[:, m, 0, :], weighted[:, m, 2, :], ADD)

@@ -11,7 +11,15 @@ W = T * JT
 U = N // W
 PAIRS = ((0, 1), (0, 2), (1, 2))
 
-GROUPS = [(r, wave - r) for wave in range(U + LAYERS - 1) for r in range(LAYERS) if 0 <= wave - r < U]
+LAST_LONG_GROUP = (0, U - 1)
+
+
+def place_in_order(group):
+    r, u = group
+    return LAYERS * (u + r) + r + (1.5 if group == LAST_LONG_GROUP else 0)
+
+
+GROUPS = sorted([(r, u) for r in range(LAYERS) for u in range(U)], key=place_in_order)
 BLOCKS = len(GROUPS) * KC
 
 PRODUCTS_LAG = 1
@@ -197,6 +205,12 @@ def tile_safnn_b_kernel(tc, xw, w0, b0, w1, b1, w2, b2, base, offs, out):
 
         def weighted_products(g, m):
             if not on_vector(g, m):
+                return
+            if g in LATE_GROUPS:
+                for terms in (slice(0, 2), slice(2, 3)):
+                    nc.vector.tensor_tensor(
+                        weighted[:, m, terms, entries_of(g)], col_rows_of[g][:, terms, :], h32_of[g][:, m, terms, :], MULT
+                    )
                 return
             nc.vector.tensor_tensor(weighted[:, m, :, entries_of(g)], col_rows_of[g][:], h32_of[g][:, m, :, :], MULT)
 

@@ -29,7 +29,7 @@ SPREAD_LAG = 8
 WEIGHTED_LAG = SPREAD_LAG + KC - 1
 SUM_LAG = WEIGHTED_LAG + 1
 
-LATE_GROUPS = range(len(GROUPS) - U, len(GROUPS))
+LATE_GROUPS = range(len(GROUPS) // 2, len(GROUPS))
 
 FLOPS = 2 * N * C * (D + 2 * C) + 2 * len(PAIRS) * C * N + 5 * C * N
 
@@ -138,7 +138,9 @@ def tile_safnn_b_kernel(tc, xw, w0, b0, w1, b1, w2, b2, base, offs, out):
                 if r < LAYERS - 1:
                     h16_of[(r, u)] = hidden16.tile([P, KC, T, JT], BF16, name="h16")
             result = acc[:].rearrange("p (j t) -> p t j" if r == 0 else "p (t j) -> p t j", t=T)
-            nc.scalar.activation(h32_of[g][:, m, :, :], result, RELU, bias=bias[r][:, m : m + 1])
+            parts = (slice(0, 2), slice(2, 3)) if g == len(GROUPS) - 1 else (slice(0, T),)
+            for part in parts:
+                nc.scalar.activation(h32_of[g][:, m, part, :], result[:, part, :], RELU, bias=bias[r][:, m : m + 1])
             if r < LAYERS - 1:
                 nc.scalar.activation(h16_of[(r, u)][:, m, :, :], result, RELU, bias=bias[r][:, m : m + 1])
 
@@ -160,10 +162,10 @@ def tile_safnn_b_kernel(tc, xw, w0, b0, w1, b1, w2, b2, base, offs, out):
             if m == 0:
                 prod_of[g] = products.tile([P, KC, len(PAIRS), JT], BF16, name="prod")
             h32, prod = h32_of[g], prod_of[g]
+            nc.vector.tensor_tensor(prod[:, m, 0, :], h32[:, m, 0, :], h32[:, m, 1, :], MULT)
             nc.vector.tensor_tensor(
-                prod[:, m, 0:2, :], h32[:, m, 0:1, :].to_broadcast([P, 2, JT]), h32[:, m, 1:3, :], MULT
+                prod[:, m, 1:3, :], h32[:, m, 0:2, :], h32[:, m, 2:3, :].to_broadcast([P, 2, JT]), MULT
             )
-            nc.vector.tensor_tensor(prod[:, m, 2, :], h32[:, m, 1, :], h32[:, m, 2, :], MULT)
 
         def scores(g):
             scores_of[g] = score_psum.tile([P, T, T, T], F32, name="scores")

@@ -77,21 +77,22 @@ def tile_safnn_b_kernel(tc, xw, w0, b0, w1, b1, w2, b2, base, offs, out):
             held.tile([P, KC, C], BF16, name="weights2"),
         ]
         samples = [held.tile([P, KD, W], BF16, name=f"samples{u}") for u in range(U)]
-        xw_blocks = xw.rearrange("(k p) n -> p k n", p=P)
+        xw_blocks = xw.rearrange("(p k) n -> p k n", p=P)
+        w0_blocks = w0.rearrange("(p k) c -> p k c", p=P)
 
         bias = []
         with nc.allow_non_contiguous_dma(reason="a bias of 512 floats, one to a partition, four blocks side by side"):
             for r, b in enumerate((b0, b1, b2)):
                 bias.append(held.tile([P, KC], F32, name=f"bias{r}"))
                 nc.gpsimd.dma_start(bias[r][:], b.rearrange("(m p) o -> p (m o)", p=P))
-        for k in range(KD):
-            nc.scalar.dma_start(weights[0][:, k, :], w0[k * P : (k + 1) * P, :])
-            nc.sync.dma_start(samples[0][:, k, :], xw[k * P : (k + 1) * P, 0:W])
+        for k in (slice(0, 1), slice(1, 2), slice(2, 4), slice(4, 6), slice(6, 8)):
+            nc.scalar.dma_start(weights[0][:, k, :], w0_blocks[:, k, :])
+            nc.sync.dma_start(samples[0][:, k, :], xw_blocks[:, k, 0:W])
         table_warmer = held.tile([P, 1], F32, name="table_warmer")
         nc.gpsimd.memset(table_warmer[:], 0.0)
         nc.scalar.activation(table_warmer[:], table_warmer[:], EXP)
-        for k in range(KD):
-            nc.sync.dma_start(samples[1][:, k, :], xw[k * P : (k + 1) * P, W : 2 * W])
+        for k in range(0, KD, 2):
+            nc.sync.dma_start(samples[1][:, k : k + 2, :], xw_blocks[:, k : k + 2, W : 2 * W])
         nc.sync.dma_start(weights[1][:], w1.rearrange("(k p) c -> p k c", p=P))
         nc.sync.dma_start(samples[2][:], xw_blocks[:, :, 2 * W : 3 * W])
         nc.sync.dma_start(weights[2][:], w2.rearrange("(k p) c -> p k c", p=P))

@@ -23,9 +23,9 @@ GROUPS = sorted([(r, u) for r in range(LAYERS) for u in range(U)], key=place_in_
 BLOCKS = len(GROUPS) * KC
 
 PRODUCTS_LAG = 1
-SCORES_LAG = 4
-SOFTMAX_LAG = 4
-SPREAD_LAG = 8
+SCORES_LAG = 6
+SOFTMAX_LAG = 6
+SPREAD_LAG = 10
 WEIGHTED_LAG = SPREAD_LAG + KC - 1
 SUM_LAG = WEIGHTED_LAG + 1
 

@@ -88,9 +88,6 @@ def tile_safnn_b_kernel(tc, xw, w0, b0, w1, b1, w2, b2, base, offs, out):
         for k in (slice(0, 1), slice(1, 2), slice(2, 4), slice(4, 6), slice(6, 8)):
             nc.scalar.dma_start(weights[0][:, k, :], w0_blocks[:, k, :])
             nc.sync.dma_start(samples[0][:, k, :], xw_blocks[:, k, 0:W])
-        table_warmer = held.tile([P, 1], F32, name="table_warmer")
-        nc.gpsimd.memset(table_warmer[:], 0.0)
-        nc.scalar.activation(table_warmer[:], table_warmer[:], EXP)
         for k in range(0, KD, 2):
             nc.sync.dma_start(samples[1][:, k : k + 2, :], xw_blocks[:, k : k + 2, W : 2 * W])
         nc.sync.dma_start(weights[1][:], w1.rearrange("(k p) c -> p k c", p=P))
@@ -139,7 +136,7 @@ def tile_safnn_b_kernel(tc, xw, w0, b0, w1, b1, w2, b2, base, offs, out):
                 if r < LAYERS - 1:
                     h16_of[(r, u)] = hidden16.tile([P, KC, T, JT], BF16, name="h16")
             result = acc[:].rearrange("p (j t) -> p t j" if r == 0 else "p (t j) -> p t j", t=T)
-            parts = (slice(0, 2), slice(2, 3)) if g == len(GROUPS) - 1 else (slice(0, T),)
+            parts = (slice(0, 2), slice(2, 3)) if (g, m) == (len(GROUPS) - 1, KC - 1) else (slice(0, T),)
             for part in parts:
                 nc.scalar.activation(h32_of[g][:, m, part, :], result[:, part, :], RELU, bias=bias[r][:, m : m + 1])
             if r < LAYERS - 1:

import concourse.masks as masks
import concourse.mybir as mybir

P = 128
D, C, N, S, T = 1024, 512, 1536, 3072, 3
LAYERS = 3
KD = D // P
KC = C // P
JT = P
W = T * JT
U = N // W
PAIRS = ((0, 1), (0, 2), (1, 2))

LAST_LONG_GROUP = (0, U - 1)


def place_in_order(group):
    r, u = group
    return LAYERS * (u + r) + r + (1.5 if group == LAST_LONG_GROUP else 0)


GROUPS = sorted([(r, u) for r in range(LAYERS) for u in range(U)], key=place_in_order)
BLOCKS = len(GROUPS) * KC

PRODUCTS_LAG = 1
SCORES_LAG = 6
SOFTMAX_LAG = 6
SPREAD_LAG = 10
WEIGHTED_LAG = SPREAD_LAG + KC - 1
SUM_LAG = WEIGHTED_LAG + 1

LATE_GROUPS = range(len(GROUPS) // 2, len(GROUPS))

FLOPS = 2 * N * C * (D + 2 * C) + 2 * len(PAIRS) * C * N + 5 * C * N

BF16, F32, U16 = mybir.dt.bfloat16, mybir.dt.float32, mybir.dt.uint16
ADD, SUBTRACT, MULT = mybir.AluOpType.add, mybir.AluOpType.subtract, mybir.AluOpType.mult
RELU, EXP = mybir.ActivationFunctionType.Relu, mybir.ActivationFunctionType.Exp
COPY = mybir.ActivationFunctionType.Copy
X = mybir.AxisListType.X

SOFTMAX_TILES = {
    "expd": [P, T, T, T],
    "total": [P, T, T],
    "att": [P, T, T],
    "col": [P, T],
}


def for_block(block, stage):
    if 0 <= block < BLOCKS:
        stage(*divmod(block, KC))


def for_group_ending_at(block, stage):
    g, m = divmod(block, KC)
    if m == KC - 1 and 0 <= g < len(GROUPS):
        stage(g)


def tile_safnn_b_kernel(tc, xw, w0, b0, w1, b1, w2, b2, base, offs, out):
    nc = tc.nc
    with (
        tc.tile_pool(name="held", bufs=1) as held,
        tc.tile_pool(name="hidden32", bufs=6) as hidden32,
        tc.tile_pool(name="hidden16", bufs=6) as hidden16,
        tc.tile_pool(name="products", bufs=3) as products,
        tc.tile_pool(name="small", bufs=len(LATE_GROUPS) + 1) as small,
        tc.tile_pool(name="turned", bufs=3) as turned,
        tc.psum_pool(name="layer_psum", bufs=5) as layer_psum,
        tc.psum_pool(name="score_psum", bufs=1) as score_psum,
        tc.psum_pool(name="weight_psum", bufs=2) as weight_psum,
    ):
        weights = [
            held.tile([P, KD, C], BF16, name="weights0"),
            held.tile([P, KC, C], BF16, name="weights1"),
            held.tile([P, KC, C], BF16, name="weights2"),
        ]
        samples = [held.tile([P, KD, W], BF16, name=f"samples{u}") for u in range(U)]
        xw_blocks = xw.rearrange("(p k) n -> p k n", p=P)
        w0_blocks = w0.rearrange("(p k) c -> p k c", p=P)

        bias = []
        with nc.allow_non_contiguous_dma(reason="a bias of 512 floats, one to a partition, four blocks side by side"):
            for r, b in enumerate((b0, b1, b2)):
                bias.append(held.tile([P, KC], F32, name=f"bias{r}"))
                nc.gpsimd.dma_start(bias[r][:], b.rearrange("(m p) o -> p (m o)", p=P))
        for k in (slice(0, 1), slice(1, 2), slice(2, 4), slice(4, 6), slice(6, 8)):
            nc.scalar.dma_start(weights[0][:, k, :], w0_blocks[:, k, :])
            nc.sync.dma_start(samples[0][:, k, :], xw_blocks[:, k, 0:W])
        for k in range(0, KD, 2):
            nc.sync.dma_start(samples[1][:, k : k + 2, :], xw_blocks[:, k : k + 2, W : 2 * W])
        nc.sync.dma_start(weights[1][:], w1.rearrange("(k p) c -> p k c", p=P))
        nc.sync.dma_start(samples[2][:], xw_blocks[:, :, 2 * W : 3 * W])
        nc.sync.dma_start(weights[2][:], w2.rearrange("(k p) c -> p k c", p=P))
        nc.sync.dma_start(samples[3][:], xw_blocks[:, :, 3 * W : 4 * W])

        offsets = held.tile([P, N // 16], U16, name="offsets")
        nc.sync.dma_start(offsets[:], offs)
        window = [held.tile([P, S], F32, name=f"window{m}") for m in range(KC)]
        for m in range(KC):
            nc.sync.dma_start(window[m][:], base[m * P : (m + 1) * P, :])

        identity = held.tile([P, P], F32, name="identity")
        masks.make_identity(nc, identity[:])
        pair_places = held.tile([P, len(PAIRS), T * T], BF16, name="pair_places")
        nc.gpsimd.memset(pair_places[:], 0.0)
        for q, (i, t) in enumerate(PAIRS):
            nc.gpsimd.memset(pair_places[:, q, T * i + t : T * i + t + 1], 1.0)
            nc.gpsimd.memset(pair_places[:, q, T * t + i : T * t + i + 1], 1.0)
        difference_places = held.tile([P, len(PAIRS) * T, T, T], BF16, name="difference_places")
        places_by_row = pair_places[:].rearrange("p q (i u) -> p (q i) u", u=T)
        nc.gpsimd.tensor_tensor(
            difference_places[:],
            places_by_row.unsqueeze(2).to_broadcast([P, len(PAIRS) * T, T, T]),
            places_by_row.unsqueeze(3).to_broadcast([P, len(PAIRS) * T, T, T]),
            SUBTRACT,
        )

        weighted = held.tile([P, KC, T, N], F32, name="weighted")

        h32_of, h16_of, prod_of, scores_of, soft_of, col_rows_of = {}, {}, {}, {}, {}, {}

        def multiply(g, m, acc, k):
            r, u = GROUPS[g]
            moving = samples[u] if r == 0 else h16_of[(r - 1, u)][:].rearrange("p k t j -> p k (t j)")
            last = (KD if r == 0 else KC) - 1
            nc.tensor.matmul(
                acc[:], weights[r][:, k, m * P : (m + 1) * P], moving[:, k, :], start=(k == 0), stop=(k == last)
            )

        def bias_and_relu(g, m, acc):
            r, u = GROUPS[g]
            if m == 0:
                h32_of[g] = hidden32.tile([P, KC, T, JT], F32, name="h32")
                if r < LAYERS - 1:
                    h16_of[(r, u)] = hidden16.tile([P, KC, T, JT], BF16, name="h16")
            result = acc[:].rearrange("p (j t) -> p t j" if r == 0 else "p (t j) -> p t j", t=T)
            parts = (slice(0, 2), slice(2, 3)) if (g, m) == (len(GROUPS) - 1, KC - 1) else (slice(0, T),)
            for part in parts:
                nc.scalar.activation(h32_of[g][:, m, part, :], result[:, part, :], RELU, bias=bias[r][:, m : m + 1])
            if r < LAYERS - 1:
                nc.scalar.activation(h16_of[(r, u)][:, m, :, :], result, RELU, bias=bias[r][:, m : m + 1])

        def layer_block(g, m):
            acc = layer_psum.tile([P, W], F32, name="acc")
            for k in range(KD if GROUPS[g][0] == 0 else KC):
                multiply(g, m, acc, k)
            bias_and_relu(g, m, acc)

        def first_group():
            accs = [layer_psum.tile([P, W], F32, name="acc") for m in range(KC)]
            for k in range(KD):
                for m in range(KC):
                    multiply(0, m, accs[m], k)
            for m in range(KC):
                bias_and_relu(0, m, accs[m])

        def pair_products(g, m):
            if m == 0:
                prod_of[g] = products.tile([P, KC, len(PAIRS), JT], BF16, name="prod")
            h32, prod = h32_of[g], prod_of[g]
            nc.vector.tensor_tensor(prod[:, m, 0, :], h32[:, m, 0, :], h32[:, m, 1, :], MULT)
            nc.vector.tensor_tensor(
                prod[:, m, 1:3, :], h32[:, m, 0:2, :], h32[:, m, 2:3, :].to_broadcast([P, 2, JT]), MULT
            )

        def scores(g):
            scores_of[g] = score_psum.tile([P, T, T, T], F32, name="scores")
            for m in range(KC):
                for q in range(len(PAIRS)):
                    nc.tensor.matmul(
                        scores_of[g][:].rearrange("p i t u -> p (i t u)"),
                        prod_of[g][:, m, q, :],
                        difference_places[:, q * T : (q + 1) * T, :, :].rearrange("p i t u -> p (i t u)"),
                        start=(m == 0 and q == 0),
                        stop=(m == KC - 1 and q == len(PAIRS) - 1),
                    )

        def exponentials(g):
            soft_of[g] = {name: small.tile(shape, F32, name=name) for name, shape in SOFTMAX_TILES.items()}
            nc.scalar.activation(soft_of[g]["expd"][:], scores_of[g][:], EXP)

        def denominators(g):
            nc.vector.reduce_sum(soft_of[g]["total"][:], soft_of[g]["expd"][:], axis=X)

        def attention(g):
            nc.vector.reciprocal(soft_of[g]["att"][:], soft_of[g]["total"][:])

        def column_sums(g):
            nc.vector.reduce_sum(soft_of[g]["col"][:], soft_of[g]["att"][:].rearrange("p i t -> p t i"), axis=X)

        def spread(g):
            col_rows_of[g] = weight_psum.tile([P, T, JT], F32, name="col_rows")
            col = soft_of[g]["col"]
            for t in range(T):
                nc.tensor.transpose(col_rows_of[g][:, t, :], col[:, t : t + 1].to_broadcast([P, P]), identity[:])

        def entries_of(g):
            r, u = GROUPS[g]
            return slice((r * U + u) * JT, (r * U + u + 1) * JT)

        def on_vector(g, m):
            return m == 0 or g not in LATE_GROUPS

        def weighted_products(g, m):
            if not on_vector(g, m):
                return
            if g in LATE_GROUPS:
                for terms in (slice(0, 2), slice(2, 3)):
                    nc.vector.tensor_tensor(
                        weighted[:, m, terms, entries_of(g)], col_rows_of[g][:, terms, :], h32_of[g][:, m, terms, :], MULT
                    )
                return
            nc.vector.tensor_tensor(weighted[:, m, :, entries_of(g)], col_rows_of[g][:], h32_of[g][:, m, :, :], MULT)

        def weighted_sum(g):
            blocks = slice(0, 1) if g in LATE_GROUPS else slice(0, KC)
            first, second = weighted[:, blocks, 0, entries_of(g)], weighted[:, blocks, 1, entries_of(g)]
            nc.vector.tensor_tensor(first, first, second, ADD)

        for turn in range(BLOCKS + SUM_LAG):
            for_group_ending_at(turn - SPREAD_LAG, spread)
            for_group_ending_at(turn - SCORES_LAG, scores)
            for_group_ending_at(turn - SOFTMAX_LAG, exponentials)
            for_group_ending_at(turn - SOFTMAX_LAG - 1, attention)
            for_group_ending_at(turn - SUM_LAG, weighted_sum)
            for_block(turn - PRODUCTS_LAG, pair_products)
            for_group_ending_at(turn - SOFTMAX_LAG, denominators)
            for_group_ending_at(turn - SOFTMAX_LAG - 1, column_sums)
            for_block(turn - WEIGHTED_LAG, weighted_products)
            if turn == 0:
                first_group()
            elif turn >= KC:
                for_block(turn, layer_block)

        scaled_of = {}

        def turn_and_scale(g, m):
            rows = layer_psum.tile([P, T, P], F32, name="rows", tag="acc")
            for t in range(T):
                nc.tensor.transpose(rows[:, t, :], h32_of[g][:, m, t, :], identity[:])
            scaled_of[(g, m)] = turned.tile([P, T, P], F32, name="scaled")
            for t in range(T):
                nc.scalar.activation(
                    scaled_of[(g, m)][:, t, :], rows[:, t, :], COPY, scale=soft_of[g]["col"][:, t : t + 1]
                )

        def turn_back_and_add(g, m):
            sums = layer_psum.tile([P, 2, JT], F32, name="sums", tag="acc")
            scaled = scaled_of[(g, m)]
            nc.tensor.matmul(sums[:, 0, :], scaled[:, 0, :], identity[:], start=True, stop=False)
            nc.tensor.matmul(sums[:, 0, :], scaled[:, 1, :], identity[:], start=False, stop=True)
            nc.tensor.matmul(sums[:, 1, :], scaled[:, 2, :], identity[:], start=True, stop=True)
            nc.scalar.activation(weighted[:, m, 0::2, entries_of(g)], sums[:], COPY)

        late_blocks = [(g, m) for m in range(1, KC) for g in LATE_GROUPS]
        for i in range(len(late_blocks) + 1):
            if i < len(late_blocks):
                turn_and_scale(*late_blocks[i])
            if i > 0:
                turn_back_and_add(*late_blocks[i - 1])

        for m in range(KC):
            nc.vector.tensor_tensor(window[m][:].indirect(offsets[:]), weighted[:, m, 0, :], weighted[:, m, 2, :], ADD)
            nc.sync.dma_start(out[m * P : (m + 1) * P, :], window[m][:])
